import numpy as np
import ml_dtypes


def mxq(x, axis, fmt="e4m3"):
    dtype, down = {"e4m3": (ml_dtypes.float8_e4m3fn, 7), "e5m2": (ml_dtypes.float8_e5m2, 14)}[fmt]
    v = np.moveaxis(np.asarray(x, np.float32).astype(ml_dtypes.bfloat16).astype(np.float64), axis, -1)
    blocks = v.reshape(v.shape[:-1] + (-1, 32))
    amax = np.abs(blocks).max(-1, keepdims=True)
    byte = np.maximum(np.where(amax > 0, np.frexp(amax)[1] - 1 + 127, 0) - down, 1)
    scale = np.exp2(byte - 127.0)
    codes = (blocks / scale).astype(np.float32).astype(dtype).astype(np.float64)
    return np.moveaxis((codes * scale).reshape(v.shape), -1, axis)


WIDE = False


def mx_kscale(k):
    if not WIDE:
        return np.ones(k)
    levels = np.array([10, -10, 5, -5, 0])
    a = np.random.permutation(np.resize(levels, k // 512 * 4)).reshape(k // 512, 4)
    idx = np.arange(k)
    return np.exp2(a[idx // 512, idx % 128 // 32])


BF16 = ml_dtypes.bfloat16


def bf(x):
    return np.asarray(x, np.float32).astype(BF16)


def f64(x):
    return np.asarray(x).astype(np.float64)


B, S, DIM, H, DH, DV, R = 2, 512, 2048, 16, 128, 128, 512
EPS = 1e-6
N = H * (DH + DV)


def rmsnorm(c, w):
    norm = np.mean(c * c, axis=-1, keepdims=True)
    return w * (c * (1.0 / np.sqrt(norm + EPS)))


def setup_inputs():
    s, t = mx_kscale(DIM), mx_kscale(R)
    return {"x": bf(np.random.standard_normal((B, S, DIM)) * s),
            "wkv_a_w": bf(np.random.standard_normal((R, DIM)) / np.sqrt(DIM) / s[None, :]),
            "wkv_a_b": bf(np.random.standard_normal(R) * 0.3),
            "kv_norm_w": bf((1.0 + 0.1 * np.random.standard_normal(R)) * t),
            "wkv_b_w": bf(np.random.standard_normal((N, R)) / np.sqrt(R) / t[None, :]),
            "wkv_b_b": bf(np.random.standard_normal(N) * 0.3)}


def reference(x, wkv_a_w, wkv_a_b, kv_norm_w, wkv_b_w, wkv_b_b):
    c = (mxq(f64(x), 2, "e4m3") @ mxq(f64(wkv_a_w), 1, "e4m3").T) + f64(wkv_a_b)
    kv_c = rmsnorm(c, f64(kv_norm_w))
    kv = (mxq(kv_c, 2, "e4m3") @ mxq(f64(wkv_b_w), 1, "e4m3").T) + f64(wkv_b_b)
    kv = kv.reshape(B, S, H, DH + DV)
    return kv[..., :DH], kv[..., DH:]

@@ -1,0 +1,301 @@
+from contextlib import ExitStack
+
+import concourse.mybir as mybir
+from concourse.masks import make_identity
+
+F32 = mybir.dt.float32
+BF16 = mybir.dt.bfloat16
+U32 = mybir.dt.uint32
+U8 = mybir.dt.uint8
+FP8X4 = mybir.dt.float8_e4m3fn_x4
+ALU = mybir.AluOpType
+ACT = mybir.ActivationFunctionType
+
+P = 128
+PACK = 4
+K_PASS = P * PACK
+TOKENS = 2 * 512
+DIM = 2048
+RANK = 512
+HEADS = 16
+HEAD_COLS = 128
+EPS = 1e-6
+
+TOKEN_TILES = TOKENS // P
+PASSES_A = DIM // K_PASS
+BANK_COLS = 512
+PSUM_BANKS = 8
+BLOCKS = BANK_COLS // P
+CHUNKS = 2 * HEADS * HEAD_COLS // BANK_COLS
+CHUNKS_PER_OUTPUT = CHUNKS // 2
+CHUNKS_PER_STORE = 2
+UNIT = BLOCKS * K_PASS
+X_AHEAD = 3
+C_AHEAD = 2
+WB_AHEAD = 2
+SCALAR_SHARE = 4
+ROW_BIAS_A = CHUNKS
+ROW_GAIN = CHUNKS + 1
+
+FLOPS = 2 * TOKENS * DIM * RANK + 2 * TOKENS * RANK * 2 * HEADS * HEAD_COLS
+
+
+def tile_mla_pa_kernel(
+    tc, x, wkv_a_w, wkv_a_b, kv_norm_w, wkv_b_w, wkv_b_b, out_0, out_1
+):
+    nc = tc.nc
+    with ExitStack() as ctx:
+        const = ctx.enter_context(tc.tile_pool(name="const", bufs=1))
+        raw = ctx.enter_context(tc.tile_pool(name="raw", bufs=1))
+        keep = ctx.enter_context(tc.tile_pool(name="keep", bufs=1))
+        stage = ctx.enter_context(tc.tile_pool(name="stage", bufs=4))
+        norm = ctx.enter_context(tc.tile_pool(name="norm", bufs=3))
+        result = ctx.enter_context(tc.tile_pool(name="result", bufs=6))
+        psum = ctx.enter_context(tc.psum_pool(name="psum", bufs=PSUM_BANKS))
+        ctx.enter_context(tc.manual_schedule())
+
+        x_tiles = x.rearrange("b s d -> (b s) d").rearrange("(m p) d -> m p d", p=P)
+        wa_passes = wkv_a_w.rearrange("(i n) (j k) -> j n i k", n=P, k=K_PASS)
+        wb_chunks = wkv_b_w.rearrange("(g i s n) k -> s g n i k", i=BLOCKS, s=2, n=HEAD_COLS)
+        bias_b_rows = wkv_b_b.rearrange("(g i s n) -> s g i n", i=BLOCKS, s=2, n=HEAD_COLS)
+        outputs = [
+            o.rearrange("b s h n -> (b s) (h n)").rearrange("(m p) c -> m p c", p=P)
+            for o in (out_0, out_1)
+        ]
+
+        ident_f32 = const.tile([P, P], F32)
+        make_identity(nc, ident_f32[:])
+        ident_bf16 = const.tile([P, P], BF16)
+        make_identity(nc, ident_bf16[:])
+        eps = const.tile([P, 1], F32)
+        nc.vector.memset(eps[:], EPS)
+
+        vector_rows = const.tile([P, BANK_COLS], BF16)
+        nc.vector.memset(vector_rows[:], 0.0)
+        nc.scalar.dma_start(
+            out=vector_rows[ROW_BIAS_A : ROW_BIAS_A + 1, :],
+            in_=wkv_a_b.rearrange("(o r) -> o r", o=1),
+        )
+        nc.scalar.dma_start(
+            out=vector_rows[ROW_GAIN : ROW_GAIN + 1, :],
+            in_=kv_norm_w.rearrange("(o r) -> o r", o=1),
+        )
+        for s in range(2):
+            nc.scalar.dma_start(
+                out=vector_rows[
+                    s * CHUNKS_PER_OUTPUT : (s + 1) * CHUNKS_PER_OUTPUT, :
+                ].rearrange("g (i n) -> g i n", n=HEAD_COLS),
+                in_=bias_b_rows[s],
+            )
+
+        x_raw = [raw.tile([P, UNIT], BF16, name="x_raw%d" % m) for m in range(TOKEN_TILES)]
+        wa_raw = [raw.tile([P, UNIT], BF16, name="wa_raw%d" % j) for j in range(PASSES_A)]
+        wb_raw = [raw.tile([P, UNIT], BF16, name="wb_raw%d" % c) for c in range(CHUNKS)]
+
+        def load_x(m):
+            nc.sync.dma_start(out=x_raw[m][:], in_=x_tiles[m])
+
+        def load_blocks(tile, blocks):
+            nc.sync.dma_start(out=tile[:].rearrange("n (i k) -> n i k", i=BLOCKS), in_=blocks)
+
+        def load_wb(c):
+            load_blocks(wb_raw[c], wb_chunks[c // CHUNKS_PER_OUTPUT, c % CHUNKS_PER_OUTPUT])
+
+        load_x(0)
+        for j in range(PASSES_A):
+            load_blocks(wa_raw[j], wa_passes[j])
+        for m in range(1, X_AHEAD):
+            load_x(m)
+        for c in range(WB_AHEAD):
+            load_wb(c)
+        load_x(X_AHEAD)
+        for c in range(WB_AHEAD, CHUNKS):
+            load_wb(c)
+        for m in range(X_AHEAD + 1, TOKEN_TILES):
+            load_x(m)
+
+        def spread_row(row, dest):
+            nc.tensor.matmul(
+                out=dest,
+                lhsT=ident_bf16[:, row : row + 1].to_broadcast([P, P]),
+                rhs=vector_rows[:],
+                start=True,
+                stop=True,
+            )
+
+        def spread_two_rows(first_row, name):
+            bank = psum.tile([P, 2 * BANK_COLS], BF16, tag="bank")
+            for i in range(2):
+                spread_row(first_row + i, bank[:, i * BANK_COLS : (i + 1) * BANK_COLS])
+            spread = const.tile([P, 2 * BANK_COLS], BF16, name=name)
+            nc.scalar.copy(out=spread[:], in_=bank[:])
+            return spread
+
+
+        def k_onto_partitions(rows_bf16, copies):
+            words = rows_bf16.bitcast(F32).rearrange("p (j u w) -> p j u w", j=BLOCKS, u=2)
+            grouped = stage.tile([P, UNIT], BF16, tag="grouped", align_bytes=64)
+            grouped_words = grouped[:].bitcast(F32).rearrange(
+                "p (j r u) -> p j r u", j=BLOCKS, u=2
+            )
+            for half in range(2):
+                bank = psum.tile([P, 2, 2, P], F32, tag="bank")
+                for j in range(2):
+                    for u in range(2):
+                        nc.tensor.transpose(
+                            bank[:, j, u, :], words[:, 2 * half + j, u, :], ident_f32[:]
+                        )
+                copies[half](
+                    out=grouped_words[:, 2 * half : 2 * half + 2, :, :],
+                    in_=bank[:].rearrange("p j u r -> p j r u"),
+                )
+            return grouped
+
+        def quantise(grouped, name):
+            codes = keep.tile([P, BANK_COLS], U32, name=name + "_codes", align_bytes=64)
+            scales = keep.tile([P, BANK_COLS], U8, name=name + "_scales", align_bytes=64)
+            nc.vector.quantize_mx(
+                out=codes[:].bitcast(FP8X4), scales=scales[:], in_=grouped[:]
+            )
+            return codes, scales
+
+        early_copies = (nc.scalar.copy, nc.vector.tensor_copy)
+        late_copies = (nc.scalar.copy, nc.scalar.copy)
+
+        x_grouped = {}
+        x_mx = {}
+        wa_mx = {}
+        wb_grouped = {}
+        wb_mx = {}
+        c_plain = {}
+        c_gain = {}
+        kvc = {}
+        kvc_mx = {}
+
+        def first_matmul(m):
+            c_acc = psum.tile([P, RANK], F32, tag="bank")
+            for j in range(PASSES_A):
+                nc.tensor.matmul_mx(
+                    out=c_acc[:],
+                    lhsT=x_mx[m][0][:, j * P : (j + 1) * P].bitcast(FP8X4),
+                    lhsT_scale=x_mx[m][1][:, j * P : (j + 1) * P],
+                    rhs=wa_mx[j][0][:].bitcast(FP8X4),
+                    rhs_scale=wa_mx[j][1][:],
+                    start=(j == 0),
+                    stop=(j == PASSES_A - 1),
+                )
+            c_sb = norm.tile([P, RANK], F32)
+            nc.vector.tensor_tensor(out=c_sb[:], in0=c_acc[:], in1=bias_a, op=ALU.add)
+            c_times_gain = norm.tile([P, RANK], F32)
+            nc.gpsimd.tensor_tensor(out=c_times_gain[:], in0=c_sb[:], in1=gain, op=ALU.mult)
+            c_plain[m] = c_sb
+            c_gain[m] = c_times_gain
+
+        def finish_norm(m):
+            squares = norm.tile([P, RANK], BF16)
+            sum_squares = norm.tile([P, 1], F32)
+            nc.scalar.activation(
+                out=squares[:], in_=c_plain[m][:], func=ACT.Square, accum_out=sum_squares[:]
+            )
+            inv_rms = norm.tile([P, 1], F32)
+            nc.scalar.activation(
+                out=inv_rms[:],
+                in_=sum_squares[:],
+                func=ACT.Abs_reciprocal_sqrt,
+                scale=1.0 / RANK,
+                bias=eps[:],
+            )
+            kvc_bf16 = norm.tile([P, RANK], BF16)
+            nc.scalar.activation(
+                out=kvc_bf16[:].rearrange("t (u e p) -> t u e p", u=2, e=2),
+                in_=c_gain[m][:].rearrange("t (u p e) -> t u e p", u=2, e=2),
+                func=ACT.Copy,
+                scale=inv_rms[:],
+            )
+            kvc[m] = kvc_bf16
+
+        def quantise_kvc(m):
+            kvc_t = psum.tile([P, PACK, P], BF16, tag="bank")
+            for t in range(PACK):
+                nc.tensor.transpose(
+                    kvc_t[:, t, :], kvc[m][:, t * P : (t + 1) * P], ident_bf16[:]
+                )
+            kvc_grouped = norm.tile([P, P, PACK], BF16, align_bytes=64)
+            nc.scalar.copy(out=kvc_grouped[:], in_=kvc_t[:].rearrange("p t r -> p r t"))
+            codes = keep.tile([P, P], U32, name="kvc%d_codes" % m, align_bytes=64)
+            scales = keep.tile([P, P], U8, name="kvc%d_scales" % m, align_bytes=64)
+            nc.vector.quantize_mx(
+                out=codes[:].bitcast(FP8X4),
+                scales=scales[:],
+                in_=kvc_grouped[:].rearrange("p r t -> p (r t)"),
+            )
+            kvc_mx[m] = (codes, scales)
+
+        def second_matmul(m, output):
+            for first in range(0, CHUNKS_PER_OUTPUT, CHUNKS_PER_STORE):
+                kv_sb = result.tile([P, CHUNKS_PER_STORE * BANK_COLS], F32)
+                for i in range(CHUNKS_PER_STORE):
+                    c = output * CHUNKS_PER_OUTPUT + first + i
+                    prepare = c + WB_AHEAD
+                    if m == 0 and prepare < CHUNKS:
+                        wb_grouped[prepare] = k_onto_partitions(wb_raw[prepare][:], late_copies)
+                    acc = psum.tile([P, BANK_COLS], F32, tag="bank")
+                    nc.tensor.matmul_mx(
+                        out=acc[:],
+                        lhsT=kvc_mx[m][0][:].bitcast(FP8X4),
+                        lhsT_scale=kvc_mx[m][1][:],
+                        rhs=wb_mx[c][0][:].bitcast(FP8X4),
+                        rhs_scale=wb_mx[c][1][:],
+                        start=True,
+                        stop=True,
+                    )
+                    kv_cols = kv_sb[:, i * BANK_COLS : (i + 1) * BANK_COLS]
+                    bias_cols = bias_b[c // 2][:, (c % 2) * BANK_COLS : (c % 2 + 1) * BANK_COLS]
+                    if m > 0 and (m * CHUNKS + c) % SCALAR_SHARE == 1:
+                        nc.scalar.copy(out=kv_cols, in_=acc[:])
+                        nc.gpsimd.tensor_tensor(
+                            out=kv_cols, in0=kv_cols, in1=bias_cols, op=ALU.add
+                        )
+                    else:
+                        nc.vector.tensor_tensor(
+                            out=kv_cols, in0=acc[:], in1=bias_cols, op=ALU.add
+                        )
+                    if m == 0 and prepare < CHUNKS:
+                        wb_mx[prepare] = quantise(wb_grouped[prepare], "wb%d" % prepare)
+                nc.sync.dma_start(
+                    out=outputs[output][m][
+                        :, first * BANK_COLS : (first + CHUNKS_PER_STORE) * BANK_COLS
+                    ],
+                    in_=kv_sb[:],
+                )
+
+        x_mx[0] = quantise(k_onto_partitions(x_raw[0][:], early_copies), "x0")
+        bias_a_and_gain = spread_two_rows(ROW_BIAS_A, "bias_a_and_gain")
+        bias_a = bias_a_and_gain[:, 0:RANK]
+        gain = bias_a_and_gain[:, RANK : 2 * RANK]
+        bias_b = []
+        for j in range(PASSES_A):
+            wa_mx[j] = quantise(k_onto_partitions(wa_raw[j][:], early_copies), "wa%d" % j)
+            bias_b.append(spread_two_rows(2 * j, "bias_b%d" % j))
+
+        for m in range(-C_AHEAD, TOKEN_TILES):
+            ahead_x = m + X_AHEAD
+            ahead_c = m + C_AHEAD
+            copies = early_copies if m < 0 else late_copies
+            if ahead_x < TOKEN_TILES:
+                x_grouped[ahead_x] = k_onto_partitions(x_raw[ahead_x][:], copies)
+            if ahead_c < TOKEN_TILES:
+                first_matmul(ahead_c)
+            if m >= 0:
+                second_matmul(m, 0)
+            if 0 <= m + 1 < TOKEN_TILES:
+                quantise_kvc(m + 1)
+            if ahead_x < TOKEN_TILES:
+                x_mx[ahead_x] = quantise(x_grouped[ahead_x], "x%d" % ahead_x)
+            if ahead_c < TOKEN_TILES:
+                finish_norm(ahead_c)
+            if m >= 0:
+                second_matmul(m, 1)
+            if m == -1:
+                for c in range(WB_AHEAD):
+                    wb_mx[c] = quantise(k_onto_partitions(wb_raw[c][:], early_copies), "wb%d" % c)

@@ -69,19 +69,21 @@ def tile_mla_pa_kernel(
         make_identity(nc, ident_bf16[:])
         eps = const.tile([P, 1], F32)
         nc.vector.memset(eps[:], EPS)
+        warm = const.tile([P, 1], F32)
+        nc.scalar.activation(out=warm[:], in_=eps[:], func=ACT.Abs_reciprocal_sqrt)
 
         vector_rows = const.tile([P, BANK_COLS], BF16)
         nc.vector.memset(vector_rows[:], 0.0)
-        nc.scalar.dma_start(
+        nc.sync.dma_start(
             out=vector_rows[ROW_BIAS_A : ROW_BIAS_A + 1, :],
             in_=wkv_a_b.rearrange("(o r) -> o r", o=1),
         )
-        nc.scalar.dma_start(
+        nc.sync.dma_start(
             out=vector_rows[ROW_GAIN : ROW_GAIN + 1, :],
             in_=kv_norm_w.rearrange("(o r) -> o r", o=1),
         )
         for s in range(2):
-            nc.scalar.dma_start(
+            nc.sync.dma_start(
                 out=vector_rows[
                     s * CHUNKS_PER_OUTPUT : (s + 1) * CHUNKS_PER_OUTPUT, :
                 ].rearrange("g (i n) -> g i n", n=HEAD_COLS),
@@ -127,9 +129,9 @@ def tile_mla_pa_kernel(
             bank = psum.tile([P, 2 * BANK_COLS], BF16, tag="bank")
             for i in range(2):
                 spread_row(first_row + i, bank[:, i * BANK_COLS : (i + 1) * BANK_COLS])
-            spread = const.tile([P, 2 * BANK_COLS], BF16, name=name)
-            nc.scalar.copy(out=spread[:], in_=bank[:])
-            return spread
+            on_all = const.tile([P, 2 * BANK_COLS], BF16, name=name)
+            nc.scalar.copy(out=on_all[:], in_=bank[:])
+            return on_all
 
 
         def k_onto_partitions(rows_bf16, copies):
@@ -159,12 +161,24 @@ def tile_mla_pa_kernel(
             )
             return codes, scales
 
+        def prepare(units, copies, after_each=None):
+            ready = []
+            waiting = None
+            for i, (rows, name) in enumerate(units):
+                grouped = k_onto_partitions(rows[:], copies)
+                if after_each is not None:
+                    after_each(i)
+                if waiting is not None:
+                    ready.append(quantise(waiting[0], waiting[1]))
+                waiting = (grouped, name)
+            ready.append(quantise(waiting[0], waiting[1]))
+            return ready
+
         early_copies = (nc.scalar.copy, nc.vector.tensor_copy)
         late_copies = (nc.scalar.copy, nc.scalar.copy)
 
         x_grouped = {}
         x_mx = {}
-        wa_mx = {}
         wb_grouped = {}
         wb_mx = {}
         c_plain = {}
@@ -269,14 +283,19 @@ def tile_mla_pa_kernel(
                     in_=kv_sb[:],
                 )
 
-        x_mx[0] = quantise(k_onto_partitions(x_raw[0][:], early_copies), "x0")
-        bias_a_and_gain = spread_two_rows(ROW_BIAS_A, "bias_a_and_gain")
-        bias_a = bias_a_and_gain[:, 0:RANK]
-        gain = bias_a_and_gain[:, RANK : 2 * RANK]
-        bias_b = []
-        for j in range(PASSES_A):
-            wa_mx[j] = quantise(k_onto_partitions(wa_raw[j][:], early_copies), "wa%d" % j)
-            bias_b.append(spread_two_rows(2 * j, "bias_b%d" % j))
+        first_units = [(x_raw[0], "x0")] + [(wa_raw[j], "wa%d" % j) for j in range(PASSES_A)]
+        pair_rows = [ROW_BIAS_A] + [2 * i for i in range(CHUNKS // 2)]
+        spread = []
+        first_mx = prepare(
+            first_units,
+            early_copies,
+            after_each=lambda i: spread.append(spread_two_rows(pair_rows[i], "spread%d" % i)),
+        )
+        x_mx[0] = first_mx[0]
+        wa_mx = first_mx[1:]
+        bias_a = spread[0][:, 0:RANK]
+        gain = spread[0][:, RANK : 2 * RANK]
+        bias_b = spread[1:]
 
         for m in range(-C_AHEAD, TOKEN_TILES):
             ahead_x = m + X_AHEAD
@@ -297,5 +316,6 @@ def tile_mla_pa_kernel(
             if m >= 0:
                 second_matmul(m, 1)
             if m == -1:
+                first_wb = prepare([(wb_raw[c], "wb%d" % c) for c in range(WB_AHEAD)], early_copies)
                 for c in range(WB_AHEAD):
-                    wb_mx[c] = quantise(k_onto_partitions(wb_raw[c][:], early_copies), "wb%d" % c)
+                    wb_mx[c] = first_wb[c]

@@ -33,7 +33,6 @@ UNIT = BLOCKS * K_PASS
 X_AHEAD = 3
 C_AHEAD = 2
 WB_AHEAD = 2
-SCALAR_SHARE = 4
 ROW_BIAS_A = CHUNKS
 ROW_GAIN = CHUNKS + 1
 
@@ -265,15 +264,7 @@ def tile_mla_pa_kernel(
                     )
                     kv_cols = kv_sb[:, i * BANK_COLS : (i + 1) * BANK_COLS]
                     bias_cols = bias_b[c // 2][:, (c % 2) * BANK_COLS : (c % 2 + 1) * BANK_COLS]
-                    if m > 0 and (m * CHUNKS + c) % SCALAR_SHARE == 1:
-                        nc.scalar.copy(out=kv_cols, in_=acc[:])
-                        nc.gpsimd.tensor_tensor(
-                            out=kv_cols, in0=kv_cols, in1=bias_cols, op=ALU.add
-                        )
-                    else:
-                        nc.vector.tensor_tensor(
-                            out=kv_cols, in0=acc[:], in1=bias_cols, op=ALU.add
-                        )
+                    nc.vector.tensor_tensor(out=kv_cols, in0=acc[:], in1=bias_cols, op=ALU.add)
                     if m == 0 and prepare < CHUNKS:
                         wb_mx[prepare] = quantise(wb_grouped[prepare], "wb%d" % prepare)
                 nc.sync.dma_start(

@@ -32,7 +32,7 @@ CHUNKS_PER_STORE = 2
 UNIT = BLOCKS * K_PASS
 X_AHEAD = 3
 C_AHEAD = 2
-WB_AHEAD = 2
+WB_AHEAD = 4
 ROW_BIAS_A = CHUNKS
 ROW_GAIN = CHUNKS + 1
 
@@ -264,7 +264,15 @@ def tile_mla_pa_kernel(
                     )
                     kv_cols = kv_sb[:, i * BANK_COLS : (i + 1) * BANK_COLS]
                     bias_cols = bias_b[c // 2][:, (c % 2) * BANK_COLS : (c % 2 + 1) * BANK_COLS]
-                    nc.vector.tensor_tensor(out=kv_cols, in0=acc[:], in1=bias_cols, op=ALU.add)
+                    if c == CHUNKS - 1 and 0 < m < TOKEN_TILES - 1:
+                        nc.scalar.copy(out=kv_cols, in_=acc[:])
+                        nc.gpsimd.tensor_tensor(
+                            out=kv_cols, in0=kv_cols, in1=bias_cols, op=ALU.add
+                        )
+                    else:
+                        nc.vector.tensor_tensor(
+                            out=kv_cols, in0=acc[:], in1=bias_cols, op=ALU.add
+                        )
                     if m == 0 and prepare < CHUNKS:
                         wb_mx[prepare] = quantise(wb_grouped[prepare], "wb%d" % prepare)
                 nc.sync.dma_start(

@@ -51,7 +51,6 @@ def tile_mla_pa_kernel(
         norm = ctx.enter_context(tc.tile_pool(name="norm", bufs=3))
         result = ctx.enter_context(tc.tile_pool(name="result", bufs=6))
         psum = ctx.enter_context(tc.psum_pool(name="psum", bufs=PSUM_BANKS))
-        ctx.enter_context(tc.manual_schedule())
 
         x_tiles = x.rearrange("b s d -> (b s) d").rearrange("(m p) d -> m p d", p=P)
         wa_passes = wkv_a_w.rearrange("(i n) (j k) -> j n i k", n=P, k=K_PASS)

from contextlib import ExitStack

import concourse.mybir as mybir
from concourse.masks import make_identity

F32 = mybir.dt.float32
BF16 = mybir.dt.bfloat16
U32 = mybir.dt.uint32
U8 = mybir.dt.uint8
FP8X4 = mybir.dt.float8_e4m3fn_x4
ALU = mybir.AluOpType
ACT = mybir.ActivationFunctionType

P = 128
PACK = 4
K_PASS = P * PACK
TOKENS = 2 * 512
DIM = 2048
RANK = 512
HEADS = 16
HEAD_COLS = 128
EPS = 1e-6

TOKEN_TILES = TOKENS // P
PASSES_A = DIM // K_PASS
BANK_COLS = 512
PSUM_BANKS = 8
BLOCKS = BANK_COLS // P
CHUNKS = 2 * HEADS * HEAD_COLS // BANK_COLS
CHUNKS_PER_OUTPUT = CHUNKS // 2
CHUNKS_PER_STORE = 2
UNIT = BLOCKS * K_PASS
X_AHEAD = 3
C_AHEAD = 2
WB_AHEAD = 4
ROW_BIAS_A = CHUNKS
ROW_GAIN = CHUNKS + 1

FLOPS = 2 * TOKENS * DIM * RANK + 2 * TOKENS * RANK * 2 * HEADS * HEAD_COLS


def tile_mla_pa_kernel(
    tc, x, wkv_a_w, wkv_a_b, kv_norm_w, wkv_b_w, wkv_b_b, out_0, out_1
):
    nc = tc.nc
    with ExitStack() as ctx:
        const = ctx.enter_context(tc.tile_pool(name="const", bufs=1))
        raw = ctx.enter_context(tc.tile_pool(name="raw", bufs=1))
        keep = ctx.enter_context(tc.tile_pool(name="keep", bufs=1))
        stage = ctx.enter_context(tc.tile_pool(name="stage", bufs=4))
        norm = ctx.enter_context(tc.tile_pool(name="norm", bufs=3))
        result = ctx.enter_context(tc.tile_pool(name="result", bufs=6))
        psum = ctx.enter_context(tc.psum_pool(name="psum", bufs=PSUM_BANKS))

        x_tiles = x.rearrange("b s d -> (b s) d").rearrange("(m p) d -> m p d", p=P)
        wa_passes = wkv_a_w.rearrange("(i n) (j k) -> j n i k", n=P, k=K_PASS)
        wb_chunks = wkv_b_w.rearrange("(g i s n) k -> s g n i k", i=BLOCKS, s=2, n=HEAD_COLS)
        bias_b_rows = wkv_b_b.rearrange("(g i s n) -> s g i n", i=BLOCKS, s=2, n=HEAD_COLS)
        outputs = [
            o.rearrange("b s h n -> (b s) (h n)").rearrange("(m p) c -> m p c", p=P)
            for o in (out_0, out_1)
        ]

        ident_f32 = const.tile([P, P], F32)
        make_identity(nc, ident_f32[:])
        ident_bf16 = const.tile([P, P], BF16)
        make_identity(nc, ident_bf16[:])
        eps = const.tile([P, 1], F32)
        nc.vector.memset(eps[:], EPS)
        warm = const.tile([P, 1], F32)
        nc.scalar.activation(out=warm[:], in_=eps[:], func=ACT.Abs_reciprocal_sqrt)

        vector_rows = const.tile([P, BANK_COLS], BF16)
        nc.vector.memset(vector_rows[:], 0.0)
        nc.sync.dma_start(
            out=vector_rows[ROW_BIAS_A : ROW_BIAS_A + 1, :],
            in_=wkv_a_b.rearrange("(o r) -> o r", o=1),
        )
        nc.sync.dma_start(
            out=vector_rows[ROW_GAIN : ROW_GAIN + 1, :],
            in_=kv_norm_w.rearrange("(o r) -> o r", o=1),
        )
        for s in range(2):
            nc.sync.dma_start(
                out=vector_rows[
                    s * CHUNKS_PER_OUTPUT : (s + 1) * CHUNKS_PER_OUTPUT, :
                ].rearrange("g (i n) -> g i n", n=HEAD_COLS),
                in_=bias_b_rows[s],
            )

        x_raw = [raw.tile([P, UNIT], BF16, name="x_raw%d" % m) for m in range(TOKEN_TILES)]
        wa_raw = [raw.tile([P, UNIT], BF16, name="wa_raw%d" % j) for j in range(PASSES_A)]
        wb_raw = [raw.tile([P, UNIT], BF16, name="wb_raw%d" % c) for c in range(CHUNKS)]

        def load_x(m):
            nc.sync.dma_start(out=x_raw[m][:], in_=x_tiles[m])

        def load_blocks(tile, blocks):
            nc.sync.dma_start(out=tile[:].rearrange("n (i k) -> n i k", i=BLOCKS), in_=blocks)

        def load_wb(c):
            load_blocks(wb_raw[c], wb_chunks[c // CHUNKS_PER_OUTPUT, c % CHUNKS_PER_OUTPUT])

        load_x(0)
        for j in range(PASSES_A):
            load_blocks(wa_raw[j], wa_passes[j])
        for m in range(1, X_AHEAD):
            load_x(m)
        for c in range(WB_AHEAD):
            load_wb(c)
        load_x(X_AHEAD)
        for c in range(WB_AHEAD, CHUNKS):
            load_wb(c)
        for m in range(X_AHEAD + 1, TOKEN_TILES):
            load_x(m)

        def spread_row(row, dest):
            nc.tensor.matmul(
                out=dest,
                lhsT=ident_bf16[:, row : row + 1].to_broadcast([P, P]),
                rhs=vector_rows[:],
                start=True,
                stop=True,
            )

        def spread_two_rows(first_row, name):
            bank = psum.tile([P, 2 * BANK_COLS], BF16, tag="bank")
            for i in range(2):
                spread_row(first_row + i, bank[:, i * BANK_COLS : (i + 1) * BANK_COLS])
            on_all = const.tile([P, 2 * BANK_COLS], BF16, name=name)
            nc.scalar.copy(out=on_all[:], in_=bank[:])
            return on_all


        def k_onto_partitions(rows_bf16, copies):
            words = rows_bf16.bitcast(F32).rearrange("p (j u w) -> p j u w", j=BLOCKS, u=2)
            grouped = stage.tile([P, UNIT], BF16, tag="grouped", align_bytes=64)
            grouped_words = grouped[:].bitcast(F32).rearrange(
                "p (j r u) -> p j r u", j=BLOCKS, u=2
            )
            for half in range(2):
                bank = psum.tile([P, 2, 2, P], F32, tag="bank")
                for j in range(2):
                    for u in range(2):
                        nc.tensor.transpose(
                            bank[:, j, u, :], words[:, 2 * half + j, u, :], ident_f32[:]
                        )
                copies[half](
                    out=grouped_words[:, 2 * half : 2 * half + 2, :, :],
                    in_=bank[:].rearrange("p j u r -> p j r u"),
                )
            return grouped

        def quantise(grouped, name):
            codes = keep.tile([P, BANK_COLS], U32, name=name + "_codes", align_bytes=64)
            scales = keep.tile([P, BANK_COLS], U8, name=name + "_scales", align_bytes=64)
            nc.vector.quantize_mx(
                out=codes[:].bitcast(FP8X4), scales=scales[:], in_=grouped[:]
            )
            return codes, scales

        def prepare(units, copies, after_each=None):
            ready = []
            waiting = None
            for i, (rows, name) in enumerate(units):
                grouped = k_onto_partitions(rows[:], copies)
                if after_each is not None:
                    after_each(i)
                if waiting is not None:
                    ready.append(quantise(waiting[0], waiting[1]))
                waiting = (grouped, name)
            ready.append(quantise(waiting[0], waiting[1]))
            return ready

        early_copies = (nc.scalar.copy, nc.vector.tensor_copy)
        late_copies = (nc.scalar.copy, nc.scalar.copy)

        x_grouped = {}
        x_mx = {}
        wb_grouped = {}
        wb_mx = {}
        c_plain = {}
        c_gain = {}
        kvc = {}
        kvc_mx = {}

        def first_matmul(m):
            c_acc = psum.tile([P, RANK], F32, tag="bank")
            for j in range(PASSES_A):
                nc.tensor.matmul_mx(
                    out=c_acc[:],
                    lhsT=x_mx[m][0][:, j * P : (j + 1) * P].bitcast(FP8X4),
                    lhsT_scale=x_mx[m][1][:, j * P : (j + 1) * P],
                    rhs=wa_mx[j][0][:].bitcast(FP8X4),
                    rhs_scale=wa_mx[j][1][:],
                    start=(j == 0),
                    stop=(j == PASSES_A - 1),
                )
            c_sb = norm.tile([P, RANK], F32)
            nc.vector.tensor_tensor(out=c_sb[:], in0=c_acc[:], in1=bias_a, op=ALU.add)
            c_times_gain = norm.tile([P, RANK], F32)
            nc.gpsimd.tensor_tensor(out=c_times_gain[:], in0=c_sb[:], in1=gain, op=ALU.mult)
            c_plain[m] = c_sb
            c_gain[m] = c_times_gain

        def finish_norm(m):
            squares = norm.tile([P, RANK], BF16)
            sum_squares = norm.tile([P, 1], F32)
            nc.scalar.activation(
                out=squares[:], in_=c_plain[m][:], func=ACT.Square, accum_out=sum_squares[:]
            )
            inv_rms = norm.tile([P, 1], F32)
            nc.scalar.activation(
                out=inv_rms[:],
                in_=sum_squares[:],
                func=ACT.Abs_reciprocal_sqrt,
                scale=1.0 / RANK,
                bias=eps[:],
            )
            kvc_bf16 = norm.tile([P, RANK], BF16)
            nc.scalar.activation(
                out=kvc_bf16[:].rearrange("t (u e p) -> t u e p", u=2, e=2),
                in_=c_gain[m][:].rearrange("t (u p e) -> t u e p", u=2, e=2),
                func=ACT.Copy,
                scale=inv_rms[:],
            )
            kvc[m] = kvc_bf16

        def quantise_kvc(m):
            kvc_t = psum.tile([P, PACK, P], BF16, tag="bank")
            for t in range(PACK):
                nc.tensor.transpose(
                    kvc_t[:, t, :], kvc[m][:, t * P : (t + 1) * P], ident_bf16[:]
                )
            kvc_grouped = norm.tile([P, P, PACK], BF16, align_bytes=64)
            nc.scalar.copy(out=kvc_grouped[:], in_=kvc_t[:].rearrange("p t r -> p r t"))
            codes = keep.tile([P, P], U32, name="kvc%d_codes" % m, align_bytes=64)
            scales = keep.tile([P, P], U8, name="kvc%d_scales" % m, align_bytes=64)
            nc.vector.quantize_mx(
                out=codes[:].bitcast(FP8X4),
                scales=scales[:],
                in_=kvc_grouped[:].rearrange("p r t -> p (r t)"),
            )
            kvc_mx[m] = (codes, scales)

        def second_matmul(m, output):
            for first in range(0, CHUNKS_PER_OUTPUT, CHUNKS_PER_STORE):
                kv_sb = result.tile([P, CHUNKS_PER_STORE * BANK_COLS], F32)
                for i in range(CHUNKS_PER_STORE):
                    c = output * CHUNKS_PER_OUTPUT + first + i
                    prepare = c + WB_AHEAD
                    if m == 0 and prepare < CHUNKS:
                        wb_grouped[prepare] = k_onto_partitions(wb_raw[prepare][:], late_copies)
                    acc = psum.tile([P, BANK_COLS], F32, tag="bank")
                    nc.tensor.matmul_mx(
                        out=acc[:],
                        lhsT=kvc_mx[m][0][:].bitcast(FP8X4),
                        lhsT_scale=kvc_mx[m][1][:],
                        rhs=wb_mx[c][0][:].bitcast(FP8X4),
                        rhs_scale=wb_mx[c][1][:],
                        start=True,
                        stop=True,
                    )
                    kv_cols = kv_sb[:, i * BANK_COLS : (i + 1) * BANK_COLS]
                    bias_cols = bias_b[c // 2][:, (c % 2) * BANK_COLS : (c % 2 + 1) * BANK_COLS]
                    if c == CHUNKS - 1 and 0 < m < TOKEN_TILES - 1:
                        nc.scalar.copy(out=kv_cols, in_=acc[:])
                        nc.gpsimd.tensor_tensor(
                            out=kv_cols, in0=kv_cols, in1=bias_cols, op=ALU.add
                        )
                    else:
                        nc.vector.tensor_tensor(
                            out=kv_cols, in0=acc[:], in1=bias_cols, op=ALU.add
                        )
                    if m == 0 and prepare < CHUNKS:
                        wb_mx[prepare] = quantise(wb_grouped[prepare], "wb%d" % prepare)
                nc.sync.dma_start(
                    out=outputs[output][m][
                        :, first * BANK_COLS : (first + CHUNKS_PER_STORE) * BANK_COLS
                    ],
                    in_=kv_sb[:],
                )

        first_units = [(x_raw[0], "x0")] + [(wa_raw[j], "wa%d" % j) for j in range(PASSES_A)]
        pair_rows = [ROW_BIAS_A] + [2 * i for i in range(CHUNKS // 2)]
        spread = []
        first_mx = prepare(
            first_units,
            early_copies,
            after_each=lambda i: spread.append(spread_two_rows(pair_rows[i], "spread%d" % i)),
        )
        x_mx[0] = first_mx[0]
        wa_mx = first_mx[1:]
        bias_a = spread[0][:, 0:RANK]
        gain = spread[0][:, RANK : 2 * RANK]
        bias_b = spread[1:]

        for m in range(-C_AHEAD, TOKEN_TILES):
            ahead_x = m + X_AHEAD
            ahead_c = m + C_AHEAD
            copies = early_copies if m < 0 else late_copies
            if ahead_x < TOKEN_TILES:
                x_grouped[ahead_x] = k_onto_partitions(x_raw[ahead_x][:], copies)
            if ahead_c < TOKEN_TILES:
                first_matmul(ahead_c)
            if m >= 0:
                second_matmul(m, 0)
            if 0 <= m + 1 < TOKEN_TILES:
                quantise_kvc(m + 1)
            if ahead_x < TOKEN_TILES:
                x_mx[ahead_x] = quantise(x_grouped[ahead_x], "x%d" % ahead_x)
            if ahead_c < TOKEN_TILES:
                finish_norm(ahead_c)
            if m >= 0:
                second_matmul(m, 1)
            if m == -1:
                first_wb = prepare([(wb_raw[c], "wb%d" % c) for c in range(WB_AHEAD)], early_copies)
                for c in range(WB_AHEAD):
                    wb_mx[c] = first_wb[c]
